import numpy as np
import ml_dtypes


def mxq(x, axis, fmt="e4m3"):
    dtype, down = {"e4m3": (ml_dtypes.float8_e4m3fn, 7), "e5m2": (ml_dtypes.float8_e5m2, 14)}[fmt]
    v = np.moveaxis(np.asarray(x, np.float32).astype(ml_dtypes.bfloat16).astype(np.float64), axis, -1)
    blocks = v.reshape(v.shape[:-1] + (-1, 32))
    amax = np.abs(blocks).max(-1, keepdims=True)
    byte = np.maximum(np.where(amax > 0, np.frexp(amax)[1] - 1 + 127, 0) - down, 1)
    scale = np.exp2(byte - 127.0)
    codes = (blocks / scale).astype(np.float32).astype(dtype).astype(np.float64)
    return np.moveaxis((codes * scale).reshape(v.shape), -1, axis)


WIDE = False


def mx_kscale(k):
    if not WIDE:
        return np.ones(k)
    levels = np.array([10, -10, 5, -5, 0])
    a = np.random.permutation(np.resize(levels, k // 512 * 4)).reshape(k // 512, 4)
    idx = np.arange(k)
    return np.exp2(a[idx // 512, idx % 128 // 32])


BF16 = ml_dtypes.bfloat16


def bf(x):
    return np.asarray(x, np.float32).astype(BF16)


def f64(x):
    return np.asarray(x).astype(np.float64)


E2M1 = np.array([0.0, 0.5, 1.0, 1.5, 2.0, 3.0, 4.0, 6.0, -0.0, -0.5, -1.0, -1.5, -2.0, -3.0, -4.0, -6.0])


def pack_weight(w, fmt):
    k, n = w.shape
    w = f64(bf(w)).reshape(k // 32, 32, n)
    amax = np.abs(w).max(1)
    if fmt == "e4m3":
        byte = np.frexp(amax)[1] - 1 + 127 - 7
    else:
        mant, ex = np.frexp(amax / 6.0)
        byte = np.where(mant > 0.5, ex, ex - 1) + 127
    byte = np.clip(np.where(amax > 0, byte, 1), 1, 254)
    scaled = (w * np.exp2(127.0 - byte)[:, None, :]).reshape(k, n).astype(np.float32)
    by_word = np.ascontiguousarray(scaled.reshape(k // 512, 128, 4, n).transpose(0, 1, 3, 2))
    if fmt == "e4m3":
        words = by_word.astype(ml_dtypes.float8_e4m3fn).view(np.uint8)
    else:
        c = by_word.astype(ml_dtypes.float4_e2m1fn).view(np.uint8) & 0xF
        words = c[..., 0::2] | (c[..., 1::2] << 4)
    return np.ascontiguousarray(words), np.ascontiguousarray(byte.astype(np.uint8).reshape(k // 512, 16, n))


def unpack_weight(words, scales, fmt):
    g, p, n, _ = words.shape
    if fmt == "e4m3":
        vals = np.ascontiguousarray(words).view(ml_dtypes.float8_e4m3fn).astype(np.float64)
    else:
        nib = np.empty((g, p, n, 4), np.uint8)
        nib[..., 0::2] = words & 0xF
        nib[..., 1::2] = words >> 4
        vals = E2M1[nib]
    vals = vals * np.repeat(np.exp2(scales.astype(np.float64) - 127.0), 8, axis=1)[..., None]
    return vals.transpose(0, 1, 3, 2).reshape(g * 512, n)


B, IN, MEM, CTX, H, G = 256, 15360, 1024, 1024, 4, 3


def sigmoid(v):
    return 1.0 / (1.0 + np.exp(-v))


def setup_inputs():
    s = mx_kscale(IN)
    w = np.random.standard_normal((MEM, MEM + IN)) / np.sqrt(MEM + IN)
    w[:, MEM:] = w[:, MEM:] / s
    input_tensor = bf(np.random.standard_normal((B, IN)) * s)
    previous_memory = bf(np.random.standard_normal((B, MEM)))
    words, scales = pack_weight(np.ascontiguousarray(w.T), "e4m3")
    return {"input_tensor": input_tensor,
            "previous_memory": previous_memory,
            "fg_w_words": words,
            "fg_w_scales": scales,
            "fg_b": bf(np.random.standard_normal(MEM) * 0.3)}


def reference(input_tensor, previous_memory, fg_w_words, fg_w_scales, fg_b):
    m = f64(previous_memory)
    forget_in = np.concatenate([m, f64(input_tensor)], axis=-1)
    fgate = sigmoid((mxq(forget_in, 1, "e4m3") @ unpack_weight(fg_w_words, fg_w_scales, "e4m3")) + f64(fg_b))
    return m * fgate

@@ -1,0 +1,225 @@
+from contextlib import ExitStack
+
+import concourse.mybir as mybir
+from concourse.masks import make_identity
+
+F32 = mybir.dt.float32
+BF16 = mybir.dt.bfloat16
+I32 = mybir.dt.int32
+U32 = mybir.dt.uint32
+U8 = mybir.dt.uint8
+FP8X4 = mybir.dt.float8_e4m3fn_x4
+
+P = 128
+PACK = 4
+K_PASS = P * PACK
+BATCH = 256
+MEM = 1024
+K_ALL = 16384
+GROUPS = K_ALL // K_PASS
+M_TILES = BATCH // P
+N_HALF = 512
+N_HALVES = MEM // N_HALF
+ROUND = 4
+QUADRANTS = 4
+LIVE_ROWS = 4
+
+FLOPS = 2 * BATCH * K_ALL * MEM
+
+
+def tile_dynamicmemorycell_pa_k_kernel(
+    tc, input_tensor, previous_memory, fg_w_words, fg_w_scales, fg_b, out
+):
+    nc = tc.nc
+
+    rounds = []
+    for source, first_group in ((previous_memory, 0), (input_tensor, MEM // K_PASS)):
+        source_groups = source.shape[1] // K_PASS
+        for lo in range(0, source_groups, ROUND):
+            rounds.append((source, lo, first_group + lo, min(ROUND, source_groups - lo)))
+    n_rounds = len(rounds)
+
+    with ExitStack() as ctx:
+        keep = ctx.enter_context(tc.tile_pool(name="keep", bufs=1))
+        row_pool = ctx.enter_context(tc.tile_pool(name="rows", bufs=3))
+        sort_pool = ctx.enter_context(tc.tile_pool(name="sorted", bufs=2))
+        group_pool = ctx.enter_context(tc.tile_pool(name="grouped", bufs=2))
+        code_pool = ctx.enter_context(tc.tile_pool(name="codes", bufs=3))
+        w_pool = ctx.enter_context(tc.tile_pool(name="w", bufs=5))
+        end_pool = ctx.enter_context(tc.tile_pool(name="end", bufs=M_TILES * N_HALVES))
+        sum_pool = ctx.enter_context(tc.psum_pool(name="sums", bufs=1))
+        flip_pool = ctx.enter_context(tc.psum_pool(name="flip", bufs=ROUND))
+        ctx.enter_context(tc.manual_schedule())
+
+        copiers = (nc.scalar.copy, nc.vector.tensor_copy)
+
+        rows_of = {}
+        sorted_of = {}
+        grouped_of = {}
+        x_codes_of = {}
+        x_planes_of = {}
+        w_words_of = {}
+
+        memory = keep.tile([P, M_TILES, MEM], BF16)
+        w_planes = keep.tile([P, n_rounds, MEM], U8, align_bytes=64)
+
+        def load_rows(r):
+            source, lo, first, n = rounds[r]
+            if r == 0:
+                rows = memory
+            else:
+                rows = row_pool.tile([P, M_TILES, ROUND * K_PASS], BF16, name="rows")
+            nc.sync.dma_start(
+                out=rows[:, :, : n * K_PASS],
+                in_=source[:, lo * K_PASS : (lo + n) * K_PASS].rearrange("(m p) k -> p m k", p=P),
+            )
+            rows_of[r] = rows
+
+        def load_w_planes(r):
+            source, lo, first, n = rounds[r]
+            for quadrant in range(QUADRANTS):
+                top = 32 * quadrant
+                nc.sync.dma_start(
+                    out=w_planes[top : top + LIVE_ROWS * n, r, :].bitcast(I32),
+                    in_=fg_w_scales[
+                        first : first + n, LIVE_ROWS * quadrant : LIVE_ROWS * (quadrant + 1), :
+                    ].bitcast(I32),
+                )
+
+        def load_w_words(r):
+            source, lo, first, n = rounds[r]
+            w_words = w_pool.tile([P, ROUND, MEM], I32, name="w_words", align_bytes=64)
+            for g in range(n):
+                nc.sync.dma_start(
+                    out=w_words[:, g, :],
+                    in_=fg_w_words[first + g].rearrange("p n t -> p (n t)").bitcast(I32),
+                )
+            w_words_of[r] = w_words
+
+        def sort_words(r):
+            source, lo, first, n = rounds[r]
+            sorted_words = sort_pool.tile([P, M_TILES, ROUND, 2, P], F32, name="sorted_words")
+            for m in range(M_TILES):
+                copiers[m % 2](
+                    out=sorted_words[:, m, :n],
+                    in_=rows_of[r][:, m, : n * K_PASS]
+                    .bitcast(F32)
+                    .rearrange("q (g p u) -> q g u p", p=P, u=2),
+                )
+            sorted_of[r] = sorted_words
+
+        def transpose_round(r):
+            source, lo, first, n = rounds[r]
+            grouped = group_pool.tile([P, ROUND, BATCH, PACK], BF16, name="grouped", align_bytes=64)
+            for g in range(n):
+                flipped = flip_pool.tile([P, 2, BATCH], F32, name="flipped")
+                for u in range(2):
+                    for m in range(M_TILES):
+                        nc.tensor.transpose(
+                            flipped[:, u, m * P : (m + 1) * P],
+                            sorted_of[r][:, m, g, u, :],
+                            identity[:],
+                        )
+                copiers[g % 2](
+                    out=grouped[:, g].bitcast(F32), in_=flipped[:].rearrange("q u c -> q c u")
+                )
+            grouped_of[r] = grouped
+
+        def quantise_round(r):
+            source, lo, first, n = rounds[r]
+            x_codes = code_pool.tile([P, ROUND, BATCH], U32, name="x_codes", align_bytes=64)
+            x_planes = code_pool.tile([P, ROUND, BATCH], U8, name="x_planes", align_bytes=64)
+            nc.vector.quantize_mx(
+                out=x_codes[:, :n].rearrange("q g c -> q (g c)").bitcast(FP8X4),
+                scales=x_planes[:, :n].rearrange("q g c -> q (g c)"),
+                in_=grouped_of[r][:, :n].rearrange("q g c t -> q (g c t)"),
+            )
+            x_codes_of[r] = x_codes
+            x_planes_of[r] = x_planes
+
+        def multiply_round(r):
+            source, lo, first, n = rounds[r]
+            for g in range(n):
+                for m in range(M_TILES):
+                    batch_rows = slice(m * P, (m + 1) * P)
+                    for h in range(N_HALVES):
+                        columns = slice(h * N_HALF, (h + 1) * N_HALF)
+                        nc.tensor.matmul_mx(
+                            out=sums[(m, h)][:],
+                            lhsT=x_codes_of[r][:, g, batch_rows].bitcast(FP8X4),
+                            lhsT_scale=x_planes_of[r][:, g, batch_rows],
+                            rhs=w_words_of[r][:, g, columns].bitcast(FP8X4),
+                            rhs_scale=w_planes[LIVE_ROWS * g : P, r, columns],
+                            start=(first + g == 0),
+                            stop=(first + g == GROUPS - 1),
+                        )
+
+        load_rows(0)
+        load_rows(1)
+
+        bias_row = keep.tile([P, MEM], BF16)
+        nc.vector.memset(bias_row[:], 0.0)
+        nc.scalar.dma_start(out=bias_row[0:1, :], in_=fg_b.rearrange("(o n) -> o n", o=1))
+        nc.vector.memset(w_planes[:].rearrange("q r n -> q (r n)").bitcast(I32), 0)
+        ones = keep.tile([P, P], BF16)
+        nc.vector.memset(ones[:], 1.0)
+        zero = keep.tile([P, 1], F32)
+        nc.vector.memset(zero[:], 0.0)
+        half = keep.tile([P, 1], F32)
+        nc.scalar.activation(out=half[:], in_=zero[:], func=mybir.ActivationFunctionType.Sigmoid)
+        identity = keep.tile([P, P], F32)
+        make_identity(nc, identity[:])
+
+        load_w_planes(0)
+
+        sums = {}
+        for m in range(M_TILES):
+            for h in range(N_HALVES):
+                bank = sum_pool.tile([P, N_HALF], F32, name="sum_%d_%d" % (m, h))
+                sums[(m, h)] = bank
+
+        bias = keep.tile([P, MEM], F32)
+        for h in range(N_HALVES):
+            columns = slice(h * N_HALF, (h + 1) * N_HALF)
+            spread = flip_pool.tile([P, N_HALF], F32, name="spread", tag="flipped")
+            nc.tensor.matmul(spread[:], lhsT=ones[:], rhs=bias_row[:, columns], start=True, stop=True)
+            nc.vector.tensor_copy(out=bias[:, columns], in_=spread[:])
+
+        for r in range(2):
+            sort_words(r)
+            transpose_round(r)
+            quantise_round(r)
+        for r in range(n_rounds):
+            if r + 2 < n_rounds:
+                load_rows(r + 2)
+            if r + 1 < n_rounds:
+                load_w_planes(r + 1)
+            load_w_words(r)
+            if r + 2 < n_rounds:
+                sort_words(r + 2)
+            multiply_round(r)
+            if r + 2 < n_rounds:
+                transpose_round(r + 2)
+                quantise_round(r + 2)
+
+        gates = {}
+        for m in range(M_TILES):
+            for h in range(N_HALVES):
+                columns = slice(h * N_HALF, (h + 1) * N_HALF)
+                logits = end_pool.tile([P, N_HALF], F32, name="logits")
+                nc.vector.tensor_tensor(
+                    out=logits[:], in0=sums[(m, h)][:], in1=bias[:, columns], op=mybir.AluOpType.add
+                )
+                gate = end_pool.tile([P, N_HALF], F32, name="gate")
+                nc.scalar.activation(
+                    out=gate[:], in_=logits[:], func=mybir.ActivationFunctionType.Sigmoid
+                )
+                gates[(m, h)] = gate
+        for m in range(M_TILES):
+            for h in range(N_HALVES):
+                columns = slice(h * N_HALF, (h + 1) * N_HALF)
+                result = end_pool.tile([P, N_HALF], F32, name="result")
+                nc.vector.tensor_tensor(
+                    out=result[:], in0=gates[(m, h)][:], in1=memory[:, m, columns], op=mybir.AluOpType.mult
+                )
+                nc.sync.dma_start(out=out[m * P : (m + 1) * P, columns], in_=result[:])

@@ -79,11 +79,11 @@ def tile_dynamicmemorycell_pa_k_kernel(
             source, lo, first, n = rounds[r]
             for quadrant in range(QUADRANTS):
                 top = 32 * quadrant
-                nc.sync.dma_start(
-                    out=w_planes[top : top + LIVE_ROWS * n, r, :].bitcast(I32),
+                nc.gpsimd.dma_start(
+                    out=w_planes[top : top + LIVE_ROWS * n, r, :].bitcast(F32),
                     in_=fg_w_scales[
                         first : first + n, LIVE_ROWS * quadrant : LIVE_ROWS * (quadrant + 1), :
-                    ].bitcast(I32),
+                    ].bitcast(F32),
                 )
 
         def load_w_words(r):

@@ -21,6 +21,7 @@ M_TILES = BATCH // P
 N_HALF = 512
 N_HALVES = MEM // N_HALF
 ROUND = 4
+AHEAD = 2
 QUADRANTS = 4
 LIVE_ROWS = 4
 
@@ -52,6 +53,12 @@ def tile_dynamicmemorycell_pa_k_kernel(
         ctx.enter_context(tc.manual_schedule())
 
         copiers = (nc.scalar.copy, nc.vector.tensor_copy)
+
+        def half_columns(h):
+            return slice(h * N_HALF, (h + 1) * N_HALF)
+
+        all_columns = slice(0, MEM)
+        both_halves = range(N_HALVES)
 
         rows_of = {}
         sorted_of = {}
@@ -86,15 +93,18 @@ def tile_dynamicmemorycell_pa_k_kernel(
                     ].bitcast(F32),
                 )
 
-        def load_w_words(r):
+        def load_w_words(r, columns):
             source, lo, first, n = rounds[r]
-            w_words = w_pool.tile([P, ROUND, MEM], I32, name="w_words", align_bytes=64)
+            if r not in w_words_of:
+                w_words = w_pool.tile([P, ROUND, MEM], I32, name="w_words", align_bytes=64)
+                w_words_of[r] = w_words
             for g in range(n):
                 nc.sync.dma_start(
-                    out=w_words[:, g, :],
-                    in_=fg_w_words[first + g].rearrange("p n t -> p (n t)").bitcast(I32),
+                    out=w_words_of[r][:, g, columns],
+                    in_=fg_w_words[first + g, :, columns, :]
+                    .rearrange("p n t -> p (n t)")
+                    .bitcast(I32),
                 )
-            w_words_of[r] = w_words
 
         def sort_words(r):
             source, lo, first, n = rounds[r]
@@ -137,13 +147,13 @@ def tile_dynamicmemorycell_pa_k_kernel(
             x_codes_of[r] = x_codes
             x_planes_of[r] = x_planes
 
-        def multiply_round(r):
+        def multiply(r, groups, halves):
             source, lo, first, n = rounds[r]
-            for g in range(n):
+            for g in groups:
                 for m in range(M_TILES):
                     batch_rows = slice(m * P, (m + 1) * P)
-                    for h in range(N_HALVES):
-                        columns = slice(h * N_HALF, (h + 1) * N_HALF)
+                    for h in halves:
+                        columns = half_columns(h)
                         nc.tensor.matmul_mx(
                             out=sums[(m, h)][:],
                             lhsT=x_codes_of[r][:, g, batch_rows].bitcast(FP8X4),
@@ -154,8 +164,28 @@ def tile_dynamicmemorycell_pa_k_kernel(
                             stop=(first + g == GROUPS - 1),
                         )
 
-        load_rows(0)
-        load_rows(1)
+        def finish(h):
+            columns = half_columns(h)
+            gates = []
+            for m in range(M_TILES):
+                logits = end_pool.tile([P, N_HALF], F32, name="logits")
+                nc.vector.tensor_tensor(
+                    out=logits[:], in0=sums[(m, h)][:], in1=bias[:, columns], op=mybir.AluOpType.add
+                )
+                gate = end_pool.tile([P, N_HALF], F32, name="gate")
+                nc.scalar.activation(
+                    out=gate[:], in_=logits[:], func=mybir.ActivationFunctionType.Sigmoid
+                )
+                gates.append(gate)
+            for m in range(M_TILES):
+                result = end_pool.tile([P, N_HALF], F32, name="result")
+                nc.vector.tensor_tensor(
+                    out=result[:], in0=gates[m][:], in1=memory[:, m, columns], op=mybir.AluOpType.mult
+                )
+                nc.sync.dma_start(out=out[m * P : (m + 1) * P, columns], in_=result[:])
+
+        for r in range(AHEAD):
+            load_rows(r)
 
         bias_row = keep.tile([P, MEM], BF16)
         nc.vector.memset(bias_row[:], 0.0)
@@ -169,57 +199,43 @@ def tile_dynamicmemorycell_pa_k_kernel(
         nc.scalar.activation(out=half[:], in_=zero[:], func=mybir.ActivationFunctionType.Sigmoid)
         identity = keep.tile([P, P], F32)
         make_identity(nc, identity[:])
-
-        load_w_planes(0)
+        for r in range(n_rounds):
+            load_w_planes(r)
 
         sums = {}
         for m in range(M_TILES):
-            for h in range(N_HALVES):
+            for h in both_halves:
                 bank = sum_pool.tile([P, N_HALF], F32, name="sum_%d_%d" % (m, h))
                 sums[(m, h)] = bank
 
-        bias = keep.tile([P, MEM], F32)
-        for h in range(N_HALVES):
-            columns = slice(h * N_HALF, (h + 1) * N_HALF)
-            spread = flip_pool.tile([P, N_HALF], F32, name="spread", tag="flipped")
-            nc.tensor.matmul(spread[:], lhsT=ones[:], rhs=bias_row[:, columns], start=True, stop=True)
-            nc.vector.tensor_copy(out=bias[:, columns], in_=spread[:])
-
-        for r in range(2):
+        for r in range(AHEAD):
             sort_words(r)
             transpose_round(r)
             quantise_round(r)
-        for r in range(n_rounds):
-            if r + 2 < n_rounds:
-                load_rows(r + 2)
-            if r + 1 < n_rounds:
-                load_w_planes(r + 1)
-            load_w_words(r)
-            if r + 2 < n_rounds:
-                sort_words(r + 2)
-            multiply_round(r)
-            if r + 2 < n_rounds:
-                transpose_round(r + 2)
-                quantise_round(r + 2)
 
-        gates = {}
-        for m in range(M_TILES):
-            for h in range(N_HALVES):
-                columns = slice(h * N_HALF, (h + 1) * N_HALF)
-                logits = end_pool.tile([P, N_HALF], F32, name="logits")
-                nc.vector.tensor_tensor(
-                    out=logits[:], in0=sums[(m, h)][:], in1=bias[:, columns], op=mybir.AluOpType.add
-                )
-                gate = end_pool.tile([P, N_HALF], F32, name="gate")
-                nc.scalar.activation(
-                    out=gate[:], in_=logits[:], func=mybir.ActivationFunctionType.Sigmoid
-                )
-                gates[(m, h)] = gate
-        for m in range(M_TILES):
-            for h in range(N_HALVES):
-                columns = slice(h * N_HALF, (h + 1) * N_HALF)
-                result = end_pool.tile([P, N_HALF], F32, name="result")
-                nc.vector.tensor_tensor(
-                    out=result[:], in0=gates[(m, h)][:], in1=memory[:, m, columns], op=mybir.AluOpType.mult
-                )
-                nc.sync.dma_start(out=out[m * P : (m + 1) * P, columns], in_=result[:])
+        bias = keep.tile([P, MEM], F32)
+        for h in both_halves:
+            spread = flip_pool.tile([P, N_HALF], F32, name="spread", tag="flipped")
+            nc.tensor.matmul(
+                spread[:], lhsT=ones[:], rhs=bias_row[:, half_columns(h)], start=True, stop=True
+            )
+            nc.vector.tensor_copy(out=bias[:, half_columns(h)], in_=spread[:])
+
+        for r in range(n_rounds - AHEAD):
+            n = rounds[r][3]
+            load_rows(r + AHEAD)
+            load_w_words(r, all_columns)
+            sort_words(r + AHEAD)
+            multiply(r, range(0, n // 2), both_halves)
+            transpose_round(r + AHEAD)
+            multiply(r, range(n // 2, n), both_halves)
+            quantise_round(r + AHEAD)
+
+        last_rounds = range(n_rounds - AHEAD, n_rounds)
+        for h in both_halves:
+            for r in last_rounds:
+                load_w_words(r, half_columns(h))
+        for h in both_halves:
+            for r in last_rounds:
+                multiply(r, range(rounds[r][3]), (h,))
+            finish(h)

@@ -22,8 +22,13 @@ N_HALF = 512
 N_HALVES = MEM // N_HALF
 ROUND = 4
 AHEAD = 2
+W_PAIR = 2
+W_AHEAD = 9
 QUADRANTS = 4
 LIVE_ROWS = 4
+SLOTS = 4
+PACKS = GROUPS // SLOTS
+SYNC_PACKS = 3
 
 FLOPS = 2 * BATCH * K_ALL * MEM
 
@@ -33,21 +38,22 @@ def tile_dynamicmemorycell_pa_k_kernel(
 ):
     nc = tc.nc
 
-    rounds = []
-    for source, first_group in ((previous_memory, 0), (input_tensor, MEM // K_PASS)):
-        source_groups = source.shape[1] // K_PASS
-        for lo in range(0, source_groups, ROUND):
-            rounds.append((source, lo, first_group + lo, min(ROUND, source_groups - lo)))
+    rounds = [(previous_memory, 0, 0, MEM // K_PASS)]
+    lo = 0
+    while lo < input_tensor.shape[1] // K_PASS:
+        n = ROUND // 2 if lo == 0 else ROUND
+        rounds.append((input_tensor, lo, MEM // K_PASS + lo, n))
+        lo += n
     n_rounds = len(rounds)
+    chunks = [(0,), (1,), (2,)] + [(r, r + 1) for r in range(3, n_rounds, 2)]
 
     with ExitStack() as ctx:
         keep = ctx.enter_context(tc.tile_pool(name="keep", bufs=1))
-        row_pool = ctx.enter_context(tc.tile_pool(name="rows", bufs=3))
         sort_pool = ctx.enter_context(tc.tile_pool(name="sorted", bufs=2))
         group_pool = ctx.enter_context(tc.tile_pool(name="grouped", bufs=2))
         code_pool = ctx.enter_context(tc.tile_pool(name="codes", bufs=3))
-        w_pool = ctx.enter_context(tc.tile_pool(name="w", bufs=5))
-        end_pool = ctx.enter_context(tc.tile_pool(name="end", bufs=M_TILES * N_HALVES))
+        w_pool = ctx.enter_context(tc.tile_pool(name="w", bufs=W_AHEAD))
+        end_pool = ctx.enter_context(tc.tile_pool(name="end", bufs=M_TILES))
         sum_pool = ctx.enter_context(tc.psum_pool(name="sums", bufs=1))
         flip_pool = ctx.enter_context(tc.psum_pool(name="flip", bufs=ROUND))
         ctx.enter_context(tc.manual_schedule())
@@ -68,51 +74,56 @@ def tile_dynamicmemorycell_pa_k_kernel(
         w_words_of = {}
 
         memory = keep.tile([P, M_TILES, MEM], BF16)
-        w_planes = keep.tile([P, n_rounds, MEM], U8, align_bytes=64)
+        w_planes = keep.tile([P, PACKS, MEM], U8, align_bytes=64)
 
-        def load_rows(r):
-            source, lo, first, n = rounds[r]
-            if r == 0:
+        def load_rows(chunk):
+            source, lo, first, n = rounds[chunk[0]]
+            groups = sum(rounds[r][3] for r in chunk)
+            if chunk[0] == 0:
                 rows = memory
             else:
-                rows = row_pool.tile([P, M_TILES, ROUND * K_PASS], BF16, name="rows")
+                rows = keep.tile([P, M_TILES, groups * K_PASS], BF16, name="rows_%d" % chunk[0])
             nc.sync.dma_start(
-                out=rows[:, :, : n * K_PASS],
-                in_=source[:, lo * K_PASS : (lo + n) * K_PASS].rearrange("(m p) k -> p m k", p=P),
+                out=rows[:],
+                in_=source[:, lo * K_PASS : (lo + groups) * K_PASS].rearrange("(m p) k -> p m k", p=P),
             )
-            rows_of[r] = rows
+            for r in chunk:
+                rows_of[r] = (rows, rounds[r][1] - lo)
 
-        def load_w_planes(r):
-            source, lo, first, n = rounds[r]
+        def load_w_planes(pack):
+            queue, word = (nc.sync, I32) if pack < SYNC_PACKS else (nc.gpsimd, F32)
+            groups = slice(SLOTS * pack, SLOTS * (pack + 1))
             for quadrant in range(QUADRANTS):
                 top = 32 * quadrant
-                nc.gpsimd.dma_start(
-                    out=w_planes[top : top + LIVE_ROWS * n, r, :].bitcast(F32),
+                queue.dma_start(
+                    out=w_planes[top : top + LIVE_ROWS * SLOTS, pack, :].bitcast(word),
                     in_=fg_w_scales[
-                        first : first + n, LIVE_ROWS * quadrant : LIVE_ROWS * (quadrant + 1), :
-                    ].bitcast(F32),
+                        groups, LIVE_ROWS * quadrant : LIVE_ROWS * (quadrant + 1), :
+                    ].bitcast(word),
                 )
 
         def load_w_words(r, columns):
             source, lo, first, n = rounds[r]
-            if r not in w_words_of:
-                w_words = w_pool.tile([P, ROUND, MEM], I32, name="w_words", align_bytes=64)
-                w_words_of[r] = w_words
-            for g in range(n):
+            for group in range(first, first + n, W_PAIR):
+                if group not in w_words_of:
+                    w_words = w_pool.tile([P, W_PAIR, MEM], I32, name="w_words", align_bytes=64)
+                    for i in range(W_PAIR):
+                        w_words_of[group + i] = (w_words, i)
                 nc.sync.dma_start(
-                    out=w_words_of[r][:, g, columns],
-                    in_=fg_w_words[first + g, :, columns, :]
-                    .rearrange("p n t -> p (n t)")
+                    out=w_words_of[group][0][:, :, columns],
+                    in_=fg_w_words[group : group + W_PAIR, :, columns, :]
+                    .rearrange("g p n t -> p g (n t)")
                     .bitcast(I32),
                 )
 
         def sort_words(r):
             source, lo, first, n = rounds[r]
+            rows, start = rows_of[r]
             sorted_words = sort_pool.tile([P, M_TILES, ROUND, 2, P], F32, name="sorted_words")
             for m in range(M_TILES):
                 copiers[m % 2](
                     out=sorted_words[:, m, :n],
-                    in_=rows_of[r][:, m, : n * K_PASS]
+                    in_=rows[:, m, start * K_PASS : (start + n) * K_PASS]
                     .bitcast(F32)
                     .rearrange("q (g p u) -> q g u p", p=P, u=2),
                 )
@@ -150,6 +161,7 @@ def tile_dynamicmemorycell_pa_k_kernel(
         def multiply(r, groups, halves):
             source, lo, first, n = rounds[r]
             for g in groups:
+                w_words, i = w_words_of[first + g]
                 for m in range(M_TILES):
                     batch_rows = slice(m * P, (m + 1) * P)
                     for h in halves:
@@ -158,8 +170,10 @@ def tile_dynamicmemorycell_pa_k_kernel(
                             out=sums[(m, h)][:],
                             lhsT=x_codes_of[r][:, g, batch_rows].bitcast(FP8X4),
                             lhsT_scale=x_planes_of[r][:, g, batch_rows],
-                            rhs=w_words_of[r][:, g, columns].bitcast(FP8X4),
-                            rhs_scale=w_planes[LIVE_ROWS * g : P, r, columns],
+                            rhs=w_words[:, i, columns].bitcast(FP8X4),
+                            rhs_scale=w_planes[
+                                LIVE_ROWS * ((first + g) % SLOTS) : P, (first + g) // SLOTS, columns
+                            ],
                             start=(first + g == 0),
                             stop=(first + g == GROUPS - 1),
                         )
@@ -184,8 +198,8 @@ def tile_dynamicmemorycell_pa_k_kernel(
                 )
                 nc.sync.dma_start(out=out[m * P : (m + 1) * P, columns], in_=result[:])
 
-        for r in range(AHEAD):
-            load_rows(r)
+        for chunk in chunks[:AHEAD]:
+            load_rows(chunk)
 
         bias_row = keep.tile([P, MEM], BF16)
         nc.vector.memset(bias_row[:], 0.0)
@@ -199,8 +213,10 @@ def tile_dynamicmemorycell_pa_k_kernel(
         nc.scalar.activation(out=half[:], in_=zero[:], func=mybir.ActivationFunctionType.Sigmoid)
         identity = keep.tile([P, P], F32)
         make_identity(nc, identity[:])
-        for r in range(n_rounds):
-            load_w_planes(r)
+        load_w_planes(0)
+        load_rows(chunks[AHEAD])
+        for pack in range(1, PACKS):
+            load_w_planes(pack)
 
         sums = {}
         for m in range(M_TILES):
@@ -213,6 +229,21 @@ def tile_dynamicmemorycell_pa_k_kernel(
             transpose_round(r)
             quantise_round(r)
 
+        for r in range(n_rounds - 1):
+            n = rounds[r][3]
+            for chunk in chunks:
+                if chunk[0] == r + AHEAD > AHEAD:
+                    load_rows(chunk)
+            load_w_words(r, all_columns)
+            if r + AHEAD < n_rounds:
+                sort_words(r + AHEAD)
+            multiply(r, range(0, n // 2), both_halves)
+            if r + AHEAD < n_rounds:
+                transpose_round(r + AHEAD)
+            multiply(r, range(n // 2, n), both_halves)
+            if r + AHEAD < n_rounds:
+                quantise_round(r + AHEAD)
+
         bias = keep.tile([P, MEM], F32)
         for h in both_halves:
             spread = flip_pool.tile([P, N_HALF], F32, name="spread", tag="flipped")
@@ -221,21 +252,9 @@ def tile_dynamicmemorycell_pa_k_kernel(
             )
             nc.vector.tensor_copy(out=bias[:, half_columns(h)], in_=spread[:])
 
-        for r in range(n_rounds - AHEAD):
-            n = rounds[r][3]
-            load_rows(r + AHEAD)
-            load_w_words(r, all_columns)
-            sort_words(r + AHEAD)
-            multiply(r, range(0, n // 2), both_halves)
-            transpose_round(r + AHEAD)
-            multiply(r, range(n // 2, n), both_halves)
-            quantise_round(r + AHEAD)
-
-        last_rounds = range(n_rounds - AHEAD, n_rounds)
+        last = n_rounds - 1
         for h in both_halves:
-            for r in last_rounds:
-                load_w_words(r, half_columns(h))
+            load_w_words(last, half_columns(h))
         for h in both_halves:
-            for r in last_rounds:
-                multiply(r, range(rounds[r][3]), (h,))
+            multiply(last, range(rounds[last][3]), (h,))
             finish(h)

@@ -20,15 +20,20 @@ GROUPS = K_ALL // K_PASS
 M_TILES = BATCH // P
 N_HALF = 512
 N_HALVES = MEM // N_HALF
-ROUND = 4
-AHEAD = 2
+ROUND = 2
+AHEAD = 7
 W_PAIR = 2
-W_AHEAD = 9
+W_AHEAD = 8
 QUADRANTS = 4
 LIVE_ROWS = 4
 SLOTS = 4
 PACKS = GROUPS // SLOTS
-SYNC_PACKS = 3
+SYNC_PACKS = (0, 1, 2, 3, 4)
+LAST_ROUNDS = 3
+SPLIT = 2
+BIAS_AT = 3
+SINGLES = 2
+CHUNK = 2
 
 FLOPS = 2 * BATCH * K_ALL * MEM
 
@@ -38,24 +43,27 @@ def tile_dynamicmemorycell_pa_k_kernel(
 ):
     nc = tc.nc
 
-    rounds = [(previous_memory, 0, 0, MEM // K_PASS)]
-    lo = 0
-    while lo < input_tensor.shape[1] // K_PASS:
-        n = ROUND // 2 if lo == 0 else ROUND
-        rounds.append((input_tensor, lo, MEM // K_PASS + lo, n))
-        lo += n
+    rounds = []
+    for source, first_group in ((previous_memory, 0), (input_tensor, MEM // K_PASS)):
+        lo = 0
+        while lo < source.shape[1] // K_PASS:
+            n = min(ROUND if len(rounds) >= 2 else 2, source.shape[1] // K_PASS - lo)
+            rounds.append((source, lo, first_group + lo, n))
+            lo += n
     n_rounds = len(rounds)
-    chunks = [(0,), (1,), (2,)] + [(r, r + 1) for r in range(3, n_rounds, 2)]
+    chunks = [(r,) for r in range(0, SINGLES)] + [
+        tuple(range(r, min(r + CHUNK, n_rounds))) for r in range(SINGLES, n_rounds, CHUNK)
+    ]
 
     with ExitStack() as ctx:
         keep = ctx.enter_context(tc.tile_pool(name="keep", bufs=1))
         sort_pool = ctx.enter_context(tc.tile_pool(name="sorted", bufs=2))
         group_pool = ctx.enter_context(tc.tile_pool(name="grouped", bufs=2))
-        code_pool = ctx.enter_context(tc.tile_pool(name="codes", bufs=3))
+        code_pool = ctx.enter_context(tc.tile_pool(name="codes", bufs=AHEAD + 1))
         w_pool = ctx.enter_context(tc.tile_pool(name="w", bufs=W_AHEAD))
-        end_pool = ctx.enter_context(tc.tile_pool(name="end", bufs=M_TILES))
+        end_pool = ctx.enter_context(tc.tile_pool(name="end", bufs=M_TILES * 3))
         sum_pool = ctx.enter_context(tc.psum_pool(name="sums", bufs=1))
-        flip_pool = ctx.enter_context(tc.psum_pool(name="flip", bufs=ROUND))
+        flip_pool = ctx.enter_context(tc.psum_pool(name="flip", bufs=4))
         ctx.enter_context(tc.manual_schedule())
 
         copiers = (nc.scalar.copy, nc.vector.tensor_copy)
@@ -64,7 +72,13 @@ def tile_dynamicmemorycell_pa_k_kernel(
             return slice(h * N_HALF, (h + 1) * N_HALF)
 
         all_columns = slice(0, MEM)
+        halves = [half_columns(h) for h in range(N_HALVES)]
+        last_ranges = [slice(0, 512), slice(512, 768), slice(768, 1024)]
         both_halves = range(N_HALVES)
+
+        last_rounds = range(n_rounds - LAST_ROUNDS, n_rounds)
+        last_groups = range(rounds[last_rounds[0]][2], GROUPS)
+        early_groups = range(0, last_groups.start)
 
         rows_of = {}
         sorted_of = {}
@@ -91,7 +105,7 @@ def tile_dynamicmemorycell_pa_k_kernel(
                 rows_of[r] = (rows, rounds[r][1] - lo)
 
         def load_w_planes(pack):
-            queue, word = (nc.sync, I32) if pack < SYNC_PACKS else (nc.gpsimd, F32)
+            queue, word = (nc.sync, I32) if pack in SYNC_PACKS else (nc.gpsimd, F32)
             groups = slice(SLOTS * pack, SLOTS * (pack + 1))
             for quadrant in range(QUADRANTS):
                 top = 32 * quadrant
@@ -101,6 +115,12 @@ def tile_dynamicmemorycell_pa_k_kernel(
                         groups, LIVE_ROWS * quadrant : LIVE_ROWS * (quadrant + 1), :
                     ].bitcast(word),
                 )
+
+        def load_sync_packs(r):
+            first = rounds[r][2]
+            for pack in SYNC_PACKS:
+                if first <= SLOTS * pack < first + rounds[r][3]:
+                    load_w_planes(pack)
 
         def load_w_words(r, columns):
             source, lo, first, n = rounds[r]
@@ -158,48 +178,78 @@ def tile_dynamicmemorycell_pa_k_kernel(
             x_codes_of[r] = x_codes
             x_planes_of[r] = x_planes
 
-        def multiply(r, groups, halves):
+        def prepare(new_rounds):
+            for new in new_rounds:
+                sort_words(new)
+            for new in new_rounds:
+                transpose_round(new)
+            for new in new_rounds:
+                quantise_round(new)
+
+        def prepared_after(r):
+            return min(n_rounds, r + AHEAD + 1, 2 * r + 2 if r >= 0 else 1)
+
+        def multiply(r, groups, column_ranges, sums, sum_groups):
             source, lo, first, n = rounds[r]
             for g in groups:
                 w_words, i = w_words_of[first + g]
                 for m in range(M_TILES):
                     batch_rows = slice(m * P, (m + 1) * P)
-                    for h in halves:
-                        columns = half_columns(h)
+                    for c, columns in enumerate(column_ranges):
                         nc.tensor.matmul_mx(
-                            out=sums[(m, h)][:],
+                            out=sums[(m, c)][:, : columns.stop - columns.start],
                             lhsT=x_codes_of[r][:, g, batch_rows].bitcast(FP8X4),
                             lhsT_scale=x_planes_of[r][:, g, batch_rows],
                             rhs=w_words[:, i, columns].bitcast(FP8X4),
                             rhs_scale=w_planes[
                                 LIVE_ROWS * ((first + g) % SLOTS) : P, (first + g) // SLOTS, columns
                             ],
-                            start=(first + g == 0),
-                            stop=(first + g == GROUPS - 1),
+                            start=(first + g == sum_groups.start),
+                            stop=(first + g == sum_groups.stop - 1),
                         )
 
-        def finish(h):
-            columns = half_columns(h)
+        def add_bias(m, h):
+            base = keep.tile([P, N_HALF], F32, name="base_%d_%d" % (m, h))
+            nc.vector.tensor_tensor(
+                out=base[:], in0=sums[(m, h)][:], in1=bias[:, half_columns(h)], op=mybir.AluOpType.add
+            )
+            bases[(m, h)] = base
+
+        def gate_range(columns, last_sums):
+            width = columns.stop - columns.start
+            h = columns.start // N_HALF
+            inside = slice(columns.start - h * N_HALF, columns.stop - h * N_HALF)
             gates = []
             for m in range(M_TILES):
                 logits = end_pool.tile([P, N_HALF], F32, name="logits")
                 nc.vector.tensor_tensor(
-                    out=logits[:], in0=sums[(m, h)][:], in1=bias[:, columns], op=mybir.AluOpType.add
+                    out=logits[:, :width],
+                    in0=last_sums[(m, 0)][:, :width],
+                    in1=bases[(m, h)][:, inside],
+                    op=mybir.AluOpType.add,
                 )
                 gate = end_pool.tile([P, N_HALF], F32, name="gate")
                 nc.scalar.activation(
-                    out=gate[:], in_=logits[:], func=mybir.ActivationFunctionType.Sigmoid
+                    out=gate[:, :width],
+                    in_=logits[:, :width],
+                    func=mybir.ActivationFunctionType.Sigmoid,
                 )
                 gates.append(gate)
+            return gates
+
+        def store_range(columns, gates):
+            width = columns.stop - columns.start
             for m in range(M_TILES):
                 result = end_pool.tile([P, N_HALF], F32, name="result")
                 nc.vector.tensor_tensor(
-                    out=result[:], in0=gates[m][:], in1=memory[:, m, columns], op=mybir.AluOpType.mult
+                    out=result[:, :width],
+                    in0=gates[m][:, :width],
+                    in1=memory[:, m, columns],
+                    op=mybir.AluOpType.mult,
                 )
-                nc.sync.dma_start(out=out[m * P : (m + 1) * P, columns], in_=result[:])
+                nc.sync.dma_start(out=out[m * P : (m + 1) * P, columns], in_=result[:, :width])
 
-        for chunk in chunks[:AHEAD]:
-            load_rows(chunk)
+        load_rows(chunks[0])
 
         bias_row = keep.tile([P, MEM], BF16)
         nc.vector.memset(bias_row[:], 0.0)
@@ -213,48 +263,60 @@ def tile_dynamicmemorycell_pa_k_kernel(
         nc.scalar.activation(out=half[:], in_=zero[:], func=mybir.ActivationFunctionType.Sigmoid)
         identity = keep.tile([P, P], F32)
         make_identity(nc, identity[:])
-        load_w_planes(0)
-        load_rows(chunks[AHEAD])
         for pack in range(1, PACKS):
-            load_w_planes(pack)
+            if pack not in SYNC_PACKS:
+                load_w_planes(pack)
 
+        bias = keep.tile([P, MEM], F32)
+        bases = {}
         sums = {}
         for m in range(M_TILES):
             for h in both_halves:
                 bank = sum_pool.tile([P, N_HALF], F32, name="sum_%d_%d" % (m, h))
                 sums[(m, h)] = bank
 
-        for r in range(AHEAD):
-            sort_words(r)
-            transpose_round(r)
-            quantise_round(r)
+        prepare(range(0, 1))
 
-        for r in range(n_rounds - 1):
+        for r in range(n_rounds - LAST_ROUNDS):
             n = rounds[r][3]
+            new_rounds = range(prepared_after(r - 1), prepared_after(r))
             for chunk in chunks:
-                if chunk[0] == r + AHEAD > AHEAD:
+                if chunk[0] in new_rounds:
                     load_rows(chunk)
+            load_sync_packs(r)
             load_w_words(r, all_columns)
-            if r + AHEAD < n_rounds:
-                sort_words(r + AHEAD)
-            multiply(r, range(0, n // 2), both_halves)
-            if r + AHEAD < n_rounds:
-                transpose_round(r + AHEAD)
-            multiply(r, range(n // 2, n), both_halves)
-            if r + AHEAD < n_rounds:
-                quantise_round(r + AHEAD)
+            for new in new_rounds:
+                sort_words(new)
+            multiply(r, range(0, n - n // SPLIT), halves, sums, early_groups)
+            for new in new_rounds:
+                transpose_round(new)
+            multiply(r, range(n - n // SPLIT, n), halves, sums, early_groups)
+            for new in new_rounds:
+                quantise_round(new)
+            if r == BIAS_AT:
+                for h in both_halves:
+                    spread = flip_pool.tile([P, N_HALF], F32, name="spread", tag="flipped")
+                    nc.tensor.matmul(
+                        spread[:], lhsT=ones[:], rhs=bias_row[:, half_columns(h)], start=True, stop=True
+                    )
+                    nc.vector.tensor_copy(out=bias[:, half_columns(h)], in_=spread[:])
 
-        bias = keep.tile([P, MEM], F32)
-        for h in both_halves:
-            spread = flip_pool.tile([P, N_HALF], F32, name="spread", tag="flipped")
-            nc.tensor.matmul(
-                spread[:], lhsT=ones[:], rhs=bias_row[:, half_columns(h)], start=True, stop=True
-            )
-            nc.vector.tensor_copy(out=bias[:, half_columns(h)], in_=spread[:])
-
-        last = n_rounds - 1
-        for h in both_halves:
-            load_w_words(last, half_columns(h))
-        for h in both_halves:
-            multiply(last, range(rounds[last][3]), (h,))
-            finish(h)
+        for columns in last_ranges:
+            for r in last_rounds:
+                load_w_words(r, columns)
+        waiting = None
+        for columns in last_ranges:
+            if columns.start % N_HALF == 0:
+                for m in range(M_TILES):
+                    add_bias(m, columns.start // N_HALF)
+            last_sums = {}
+            for m in range(M_TILES):
+                last_bank = flip_pool.tile([P, N_HALF], F32, name="last_bank", tag="flipped")
+                last_sums[(m, 0)] = last_bank
+            for r in last_rounds:
+                multiply(r, range(rounds[r][3]), [columns], last_sums, last_groups)
+            gates = gate_range(columns, last_sums)
+            if waiting:
+                store_range(*waiting)
+            waiting = (columns, gates)
+        store_range(*waiting)

from contextlib import ExitStack

import concourse.mybir as mybir
from concourse.masks import make_identity

F32 = mybir.dt.float32
BF16 = mybir.dt.bfloat16
I32 = mybir.dt.int32
U32 = mybir.dt.uint32
U8 = mybir.dt.uint8
FP8X4 = mybir.dt.float8_e4m3fn_x4

P = 128
PACK = 4
K_PASS = P * PACK
BATCH = 256
MEM = 1024
K_ALL = 16384
GROUPS = K_ALL // K_PASS
M_TILES = BATCH // P
N_HALF = 512
N_HALVES = MEM // N_HALF
ROUND = 2
AHEAD = 7
W_PAIR = 2
W_AHEAD = 8
QUADRANTS = 4
LIVE_ROWS = 4
SLOTS = 4
PACKS = GROUPS // SLOTS
SYNC_PACKS = (0, 1, 2, 3, 4)
LAST_ROUNDS = 3
SPLIT = 2
BIAS_AT = 3
SINGLES = 2
CHUNK = 2

FLOPS = 2 * BATCH * K_ALL * MEM


def tile_dynamicmemorycell_pa_k_kernel(
    tc, input_tensor, previous_memory, fg_w_words, fg_w_scales, fg_b, out
):
    nc = tc.nc

    rounds = []
    for source, first_group in ((previous_memory, 0), (input_tensor, MEM // K_PASS)):
        lo = 0
        while lo < source.shape[1] // K_PASS:
            n = min(ROUND if len(rounds) >= 2 else 2, source.shape[1] // K_PASS - lo)
            rounds.append((source, lo, first_group + lo, n))
            lo += n
    n_rounds = len(rounds)
    chunks = [(r,) for r in range(0, SINGLES)] + [
        tuple(range(r, min(r + CHUNK, n_rounds))) for r in range(SINGLES, n_rounds, CHUNK)
    ]

    with ExitStack() as ctx:
        keep = ctx.enter_context(tc.tile_pool(name="keep", bufs=1))
        sort_pool = ctx.enter_context(tc.tile_pool(name="sorted", bufs=2))
        group_pool = ctx.enter_context(tc.tile_pool(name="grouped", bufs=2))
        code_pool = ctx.enter_context(tc.tile_pool(name="codes", bufs=AHEAD + 1))
        w_pool = ctx.enter_context(tc.tile_pool(name="w", bufs=W_AHEAD))
        end_pool = ctx.enter_context(tc.tile_pool(name="end", bufs=M_TILES * 3))
        sum_pool = ctx.enter_context(tc.psum_pool(name="sums", bufs=1))
        flip_pool = ctx.enter_context(tc.psum_pool(name="flip", bufs=4))
        ctx.enter_context(tc.manual_schedule())

        copiers = (nc.scalar.copy, nc.vector.tensor_copy)

        def half_columns(h):
            return slice(h * N_HALF, (h + 1) * N_HALF)

        all_columns = slice(0, MEM)
        halves = [half_columns(h) for h in range(N_HALVES)]
        last_ranges = [slice(0, 512), slice(512, 768), slice(768, 1024)]
        both_halves = range(N_HALVES)

        last_rounds = range(n_rounds - LAST_ROUNDS, n_rounds)
        last_groups = range(rounds[last_rounds[0]][2], GROUPS)
        early_groups = range(0, last_groups.start)

        rows_of = {}
        sorted_of = {}
        grouped_of = {}
        x_codes_of = {}
        x_planes_of = {}
        w_words_of = {}

        memory = keep.tile([P, M_TILES, MEM], BF16)
        w_planes = keep.tile([P, PACKS, MEM], U8, align_bytes=64)

        def load_rows(chunk):
            source, lo, first, n = rounds[chunk[0]]
            groups = sum(rounds[r][3] for r in chunk)
            if chunk[0] == 0:
                rows = memory
            else:
                rows = keep.tile([P, M_TILES, groups * K_PASS], BF16, name="rows_%d" % chunk[0])
            nc.sync.dma_start(
                out=rows[:],
                in_=source[:, lo * K_PASS : (lo + groups) * K_PASS].rearrange("(m p) k -> p m k", p=P),
            )
            for r in chunk:
                rows_of[r] = (rows, rounds[r][1] - lo)

        def load_w_planes(pack):
            queue, word = (nc.sync, I32) if pack in SYNC_PACKS else (nc.gpsimd, F32)
            groups = slice(SLOTS * pack, SLOTS * (pack + 1))
            for quadrant in range(QUADRANTS):
                top = 32 * quadrant
                queue.dma_start(
                    out=w_planes[top : top + LIVE_ROWS * SLOTS, pack, :].bitcast(word),
                    in_=fg_w_scales[
                        groups, LIVE_ROWS * quadrant : LIVE_ROWS * (quadrant + 1), :
                    ].bitcast(word),
                )

        def load_sync_packs(r):
            first = rounds[r][2]
            for pack in SYNC_PACKS:
                if first <= SLOTS * pack < first + rounds[r][3]:
                    load_w_planes(pack)

        def load_w_words(r, columns):
            source, lo, first, n = rounds[r]
            for group in range(first, first + n, W_PAIR):
                if group not in w_words_of:
                    w_words = w_pool.tile([P, W_PAIR, MEM], I32, name="w_words", align_bytes=64)
                    for i in range(W_PAIR):
                        w_words_of[group + i] = (w_words, i)
                nc.sync.dma_start(
                    out=w_words_of[group][0][:, :, columns],
                    in_=fg_w_words[group : group + W_PAIR, :, columns, :]
                    .rearrange("g p n t -> p g (n t)")
                    .bitcast(I32),
                )

        def sort_words(r):
            source, lo, first, n = rounds[r]
            rows, start = rows_of[r]
            sorted_words = sort_pool.tile([P, M_TILES, ROUND, 2, P], F32, name="sorted_words")
            for m in range(M_TILES):
                copiers[m % 2](
                    out=sorted_words[:, m, :n],
                    in_=rows[:, m, start * K_PASS : (start + n) * K_PASS]
                    .bitcast(F32)
                    .rearrange("q (g p u) -> q g u p", p=P, u=2),
                )
            sorted_of[r] = sorted_words

        def transpose_round(r):
            source, lo, first, n = rounds[r]
            grouped = group_pool.tile([P, ROUND, BATCH, PACK], BF16, name="grouped", align_bytes=64)
            for g in range(n):
                flipped = flip_pool.tile([P, 2, BATCH], F32, name="flipped")
                for u in range(2):
                    for m in range(M_TILES):
                        nc.tensor.transpose(
                            flipped[:, u, m * P : (m + 1) * P],
                            sorted_of[r][:, m, g, u, :],
                            identity[:],
                        )
                copiers[g % 2](
                    out=grouped[:, g].bitcast(F32), in_=flipped[:].rearrange("q u c -> q c u")
                )
            grouped_of[r] = grouped

        def quantise_round(r):
            source, lo, first, n = rounds[r]
            x_codes = code_pool.tile([P, ROUND, BATCH], U32, name="x_codes", align_bytes=64)
            x_planes = code_pool.tile([P, ROUND, BATCH], U8, name="x_planes", align_bytes=64)
            nc.vector.quantize_mx(
                out=x_codes[:, :n].rearrange("q g c -> q (g c)").bitcast(FP8X4),
                scales=x_planes[:, :n].rearrange("q g c -> q (g c)"),
                in_=grouped_of[r][:, :n].rearrange("q g c t -> q (g c t)"),
            )
            x_codes_of[r] = x_codes
            x_planes_of[r] = x_planes

        def prepare(new_rounds):
            for new in new_rounds:
                sort_words(new)
            for new in new_rounds:
                transpose_round(new)
            for new in new_rounds:
                quantise_round(new)

        def prepared_after(r):
            return min(n_rounds, r + AHEAD + 1, 2 * r + 2 if r >= 0 else 1)

        def multiply(r, groups, column_ranges, sums, sum_groups):
            source, lo, first, n = rounds[r]
            for g in groups:
                w_words, i = w_words_of[first + g]
                for m in range(M_TILES):
                    batch_rows = slice(m * P, (m + 1) * P)
                    for c, columns in enumerate(column_ranges):
                        nc.tensor.matmul_mx(
                            out=sums[(m, c)][:, : columns.stop - columns.start],
                            lhsT=x_codes_of[r][:, g, batch_rows].bitcast(FP8X4),
                            lhsT_scale=x_planes_of[r][:, g, batch_rows],
                            rhs=w_words[:, i, columns].bitcast(FP8X4),
                            rhs_scale=w_planes[
                                LIVE_ROWS * ((first + g) % SLOTS) : P, (first + g) // SLOTS, columns
                            ],
                            start=(first + g == sum_groups.start),
                            stop=(first + g == sum_groups.stop - 1),
                        )

        def add_bias(m, h):
            base = keep.tile([P, N_HALF], F32, name="base_%d_%d" % (m, h))
            nc.vector.tensor_tensor(
                out=base[:], in0=sums[(m, h)][:], in1=bias[:, half_columns(h)], op=mybir.AluOpType.add
            )
            bases[(m, h)] = base

        def gate_range(columns, last_sums):
            width = columns.stop - columns.start
            h = columns.start // N_HALF
            inside = slice(columns.start - h * N_HALF, columns.stop - h * N_HALF)
            gates = []
            for m in range(M_TILES):
                logits = end_pool.tile([P, N_HALF], F32, name="logits")
                nc.vector.tensor_tensor(
                    out=logits[:, :width],
                    in0=last_sums[(m, 0)][:, :width],
                    in1=bases[(m, h)][:, inside],
                    op=mybir.AluOpType.add,
                )
                gate = end_pool.tile([P, N_HALF], F32, name="gate")
                nc.scalar.activation(
                    out=gate[:, :width],
                    in_=logits[:, :width],
                    func=mybir.ActivationFunctionType.Sigmoid,
                )
                gates.append(gate)
            return gates

        def store_range(columns, gates):
            width = columns.stop - columns.start
            for m in range(M_TILES):
                result = end_pool.tile([P, N_HALF], F32, name="result")
                nc.vector.tensor_tensor(
                    out=result[:, :width],
                    in0=gates[m][:, :width],
                    in1=memory[:, m, columns],
                    op=mybir.AluOpType.mult,
                )
                nc.sync.dma_start(out=out[m * P : (m + 1) * P, columns], in_=result[:, :width])

        load_rows(chunks[0])

        bias_row = keep.tile([P, MEM], BF16)
        nc.vector.memset(bias_row[:], 0.0)
        nc.scalar.dma_start(out=bias_row[0:1, :], in_=fg_b.rearrange("(o n) -> o n", o=1))
        nc.vector.memset(w_planes[:].rearrange("q r n -> q (r n)").bitcast(I32), 0)
        ones = keep.tile([P, P], BF16)
        nc.vector.memset(ones[:], 1.0)
        zero = keep.tile([P, 1], F32)
        nc.vector.memset(zero[:], 0.0)
        half = keep.tile([P, 1], F32)
        nc.scalar.activation(out=half[:], in_=zero[:], func=mybir.ActivationFunctionType.Sigmoid)
        identity = keep.tile([P, P], F32)
        make_identity(nc, identity[:])
        for pack in range(1, PACKS):
            if pack not in SYNC_PACKS:
                load_w_planes(pack)

        bias = keep.tile([P, MEM], F32)
        bases = {}
        sums = {}
        for m in range(M_TILES):
            for h in both_halves:
                bank = sum_pool.tile([P, N_HALF], F32, name="sum_%d_%d" % (m, h))
                sums[(m, h)] = bank

        prepare(range(0, 1))

        for r in range(n_rounds - LAST_ROUNDS):
            n = rounds[r][3]
            new_rounds = range(prepared_after(r - 1), prepared_after(r))
            for chunk in chunks:
                if chunk[0] in new_rounds:
                    load_rows(chunk)
            load_sync_packs(r)
            load_w_words(r, all_columns)
            for new in new_rounds:
                sort_words(new)
            multiply(r, range(0, n - n // SPLIT), halves, sums, early_groups)
            for new in new_rounds:
                transpose_round(new)
            multiply(r, range(n - n // SPLIT, n), halves, sums, early_groups)
            for new in new_rounds:
                quantise_round(new)
            if r == BIAS_AT:
                for h in both_halves:
                    spread = flip_pool.tile([P, N_HALF], F32, name="spread", tag="flipped")
                    nc.tensor.matmul(
                        spread[:], lhsT=ones[:], rhs=bias_row[:, half_columns(h)], start=True, stop=True
                    )
                    nc.vector.tensor_copy(out=bias[:, half_columns(h)], in_=spread[:])

        for columns in last_ranges:
            for r in last_rounds:
                load_w_words(r, columns)
        waiting = None
        for columns in last_ranges:
            if columns.start % N_HALF == 0:
                for m in range(M_TILES):
                    add_bias(m, columns.start // N_HALF)
            last_sums = {}
            for m in range(M_TILES):
                last_bank = flip_pool.tile([P, N_HALF], F32, name="last_bank", tag="flipped")
                last_sums[(m, 0)] = last_bank
            for r in last_rounds:
                multiply(r, range(rounds[r][3]), [columns], last_sums, last_groups)
            gates = gate_range(columns, last_sums)
            if waiting:
                store_range(*waiting)
            waiting = (columns, gates)
        store_range(*waiting)
